import numpy as np
import ml_dtypes


def mxq(x, axis, fmt="e4m3"):
    dtype, down = {"e4m3": (ml_dtypes.float8_e4m3fn, 7), "e5m2": (ml_dtypes.float8_e5m2, 14)}[fmt]
    v = np.moveaxis(np.asarray(x, np.float32).astype(ml_dtypes.bfloat16).astype(np.float64), axis, -1)
    blocks = v.reshape(v.shape[:-1] + (-1, 32))
    amax = np.abs(blocks).max(-1, keepdims=True)
    byte = np.maximum(np.where(amax > 0, np.frexp(amax)[1] - 1 + 127, 0) - down, 1)
    scale = np.exp2(byte - 127.0)
    codes = (blocks / scale).astype(np.float32).astype(dtype).astype(np.float64)
    return np.moveaxis((codes * scale).reshape(v.shape), -1, axis)


WIDE = False


def mx_kscale(k):
    if not WIDE:
        return np.ones(k)
    levels = np.array([10, -10, 5, -5, 0])
    if k % 512:
        return np.exp2(np.random.permutation(np.resize(levels, k // 32))).repeat(32)
    a = np.empty((k // 512, 16))
    for p in range(k // 512):
        a[p, :8] = np.random.permutation(np.resize(levels, 8))
        for g in range(8):
            far = levels[np.abs(levels - a[p, g]) >= 10]
            a[p, g + 8] = far[np.random.randint(len(far))]
    return np.exp2(a.ravel()).repeat(32)


BF16 = ml_dtypes.bfloat16


def bf(x):
    return np.asarray(x, np.float32).astype(BF16)


def f64(x):
    return np.asarray(x).astype(np.float64)


B, S, A, O, H, L = 1024, 1024, 128, 1920, 1024, 384
K1 = S + A + O


def draw0():
    s = mx_kscale(K1)
    t = mx_kscale(H)
    col = np.concatenate([np.full(L, 0.7), np.full(L, 0.14)]) / np.sqrt(H)
    return {"prev_state": bf(np.random.standard_normal((B, S)) * s[:S]),
            "prev_action": bf(np.random.standard_normal((B, A)) * s[S:S + A]),
            "observation": bf(np.random.standard_normal((B, O)) * s[S + A:]),
            "eps": bf(np.random.standard_normal((B, L))),
            "rep_W1": bf(np.random.standard_normal((K1, H)) / np.sqrt(K1) / s[:, None] * t),
            "rep_b1": bf(np.random.standard_normal(H) * 0.1 * t),
            "rep_W2": bf(np.random.standard_normal((H, 2 * L)) * col / t[:, None]),
            "rep_b2": bf(np.concatenate([0.1 * np.random.standard_normal(L), 1.0 + 0.1 * np.random.standard_normal(L)]))}


def core(prev_state, prev_action, observation, eps, rep_W1, rep_b1, rep_W2, rep_b2):
    x = np.concatenate([f64(prev_state), f64(prev_action), f64(observation)], axis=-1)
    h1 = np.maximum((mxq(x, 1, "e4m3") @ mxq(f64(rep_W1), 0, "e4m3")) + f64(rep_b1), 0.0)
    out = (mxq(h1, 1, "e4m3") @ mxq(f64(rep_W2), 0, "e4m3")) + f64(rep_b2)
    mean, std = np.split(out, 2, axis=-1)
    sample = mean + np.sqrt(std) * f64(eps)
    return mean, std, sample


def e4m3fn_bytes(y):
    return np.clip(np.asarray(y, np.float64), -448.0, 448.0).astype(np.float32).astype(ml_dtypes.float8_e4m3fn).view(np.uint8)


def e4m3fn_values(b):
    return np.asarray(b, np.uint8).view(ml_dtypes.float8_e4m3fn).astype(np.float64)


def setup_inputs():
    d = draw0()
    x0 = np.asarray(d['observation']).astype(np.float64)
    s = (np.max(np.abs(x0), axis=(0,), keepdims=True) / 448.0).astype(np.float32)
    out = {}
    for k, v in d.items():
        if k == 'observation':
            out['observation_bytes'] = e4m3fn_bytes(x0 / s.astype(np.float64))
            out['observation_scale'] = s
        else:
            out[k] = v
    return out


def reference(prev_state, prev_action, observation_bytes, observation_scale, eps, rep_W1, rep_b1, rep_W2, rep_b2):
    return core(prev_state, prev_action, e4m3fn_values(observation_bytes) * observation_scale.astype(np.float64), eps, rep_W1, rep_b1, rep_W2, rep_b2)

@@ -1,0 +1,311 @@
+from contextlib import ExitStack
+
+import concourse.mybir as mybir
+from concourse.masks import make_identity
+
+B, S, A, O, H, L = 1024, 1024, 128, 1920, 1024, 384
+K1 = S + A + O
+FLOPS = 2 * B * K1 * H + 2 * B * H * 2 * L
+
+F32 = mybir.dt.float32
+BF16 = mybir.dt.bfloat16
+U32 = mybir.dt.uint32
+U8 = mybir.dt.uint8
+FP8 = mybir.dt.float8_e4m3fn
+FP8X4 = mybir.dt.float8_e4m3fn_x4
+ACT = mybir.ActivationFunctionType
+ALU = mybir.AluOpType
+
+P = 128
+G1 = K1 // 512
+G2 = H // 512
+NT = B // P
+
+
+def tile_rssm_pa_kernel(tc, prev_state, prev_action, obs_bytes, obs_scale, eps,
+                                    w1, b1, w2, b2, out_mean, out_std, out_sample):
+    nc = tc.nc
+
+    state_v = prev_state.rearrange("(p i) k -> p i k", i=NT)
+    action_v = prev_action.rearrange("(p i) k -> p i k", i=NT)
+    bytes_v = obs_bytes.rearrange("(p i) k -> p i k", i=NT)
+    eps_v = eps.rearrange("(p i) n -> p i n", i=NT)
+    mean_v = out_mean.rearrange("(p i) n -> p i n", i=NT)
+    std_v = out_std.rearrange("(p i) n -> p i n", i=NT)
+    sample_v = out_sample.rearrange("(p i) n -> p i n", i=NT)
+    w1_v = w1.rearrange("(g p j) c -> g p j c", p=P, j=4)
+    w2_v = w2.rearrange("(g p j) c -> g p j c", p=P, j=4)
+
+    with ExitStack() as ctx:
+        keep = ctx.enter_context(tc.tile_pool(name="keep", bufs=1))
+        rows = ctx.enter_context(tc.tile_pool(name="rows", bufs=3))
+        raw = ctx.enter_context(tc.tile_pool(name="raw", bufs=7))
+        inter = ctx.enter_context(tc.tile_pool(name="inter", bufs=8))
+        hid = ctx.enter_context(tc.tile_pool(name="hid", bufs=2))
+        outp = ctx.enter_context(tc.tile_pool(name="outp", bufs=2))
+        psum = ctx.enter_context(tc.psum_pool(name="psum", bufs=4))
+
+        ident = keep.tile([P, P], F32)
+        make_identity(nc, ident[:])
+        warm = keep.tile([P, 1], F32)
+        nc.vector.memset(warm[:], 1.0)
+        nc.scalar.activation(warm[:], warm[:], ACT.Sqrt)
+
+        w1c = keep.tile([P, G1, H], U32, align_bytes=64)
+        w1s = keep.tile([P, G1, H], U8, align_bytes=64)
+        w2c = keep.tile([P, G2, 2 * L], U32, align_bytes=64)
+        w2s = keep.tile([P, G2, 2 * L], U8, align_bytes=64)
+        scale = keep.tile([P, O], F32)
+        b1c = keep.tile([P, G2, 4], BF16)
+        b2b = keep.tile([P, 2 * L], BF16)
+        eps_sb = keep.tile([P, NT, L], BF16)
+
+        xr = {}
+        ob = {}
+        w1r = {}
+
+        def load_w1(half, g):
+            t = raw.tile([P, 4, 512], BF16, name="w1r")
+            nc.sync.dma_start(out=t[:], in_=w1_v[g][:, :, 512 * half:512 * half + 512])
+            w1r[half, g] = t
+
+        def new_rows(q):
+            xr[q] = rows.tile([P, 2, K1], BF16, name="xr", align_bytes=64)
+
+        def load_state(q, g0, g1):
+            nc.sync.dma_start(out=xr[q][:, :, 512 * g0:512 * g1],
+                              in_=state_v[:, 2 * q:2 * q + 2, 512 * g0:512 * g1])
+
+        def load_obs(q):
+            t = rows.tile([P, 2, O], U8, name="ob")
+            nc.sync.dma_start(out=t[:], in_=bytes_v[:, 2 * q:2 * q + 2, :])
+            ob[q] = t
+            nc.sync.dma_start(out=xr[q][:, :, S:S + A], in_=action_v[:, 2 * q:2 * q + 2, :])
+
+        def product(q, i, c0, c1):
+            nc.vector.tensor_tensor(out=xr[q][:, i, S + A + c0:S + A + c1],
+                                    in0=ob[q][:, i, c0:c1].bitcast(FP8),
+                                    in1=scale[:, c0:c1], op=ALU.mult)
+
+        def interleave_w1(half, g, mv):
+            t = inter.tile([P, 2048], BF16, name="il", align_bytes=64)
+            dst = t[:].rearrange("p (t m j) -> p m t j", t=4, j=4)
+            src = w1r[half, g][:].rearrange("p j (m t) -> p m t j", t=4)
+            if mv > 0:
+                nc.vector.tensor_copy(out=dst[:, :mv], in_=src[:, :mv])
+            if mv < 128:
+                nc.scalar.copy(out=dst[:, mv:], in_=src[:, mv:])
+            return t
+
+        def quant_w1(half, g, t):
+            nc.vector.quantize_mx(out=w1c[:, g, 512 * half:512 * half + 512].bitcast(FP8X4),
+                                  scales=w1s[:, g, 512 * half:512 * half + 512], in_=t[:])
+
+        class_blocks = [[0, 1], [2], [3]]
+        xc = {}
+        xs = {}
+        hc = {}
+        hs = {}
+        hp = {}
+        for b, qs in enumerate(class_blocks):
+            n = 256 * len(qs)
+            xc[b] = keep.tile([P, G1, n], U32, name="xc%d" % b, align_bytes=64)
+            xs[b] = keep.tile([P, G1, n], U8, name="xs%d" % b, align_bytes=64)
+            hc[b] = keep.tile([P, G2, n], U32, name="hc%d" % b, align_bytes=64)
+            hs[b] = keep.tile([P, G2, n], U8, name="hs%d" % b, align_bytes=64)
+
+        def x_prep(b, g, engines):
+            qs = class_blocks[b]
+            n = 256 * len(qs)
+            t = inter.tile([P, 2048], BF16, name="il", align_bytes=64)
+            words_out = t[:].bitcast(F32)
+            for h, q in enumerate(qs):
+                tp = psum.tile([P, 2, 256], F32, name="tp")
+                for i in range(2):
+                    words = xr[q][:, i, :].bitcast(F32)
+                    for u in range(2):
+                        nc.tensor.transpose(tp[:, u, 128 * i:128 * i + 128],
+                                            words[:, 256 * g + u:256 * g + 256:2], ident[:])
+                dst = words_out[:, 512 * h:512 * h + 512].rearrange("p (r u) -> p r u", u=2)
+                src = tp[:].rearrange("p u r -> p r u")
+                if engines[h] == "v":
+                    nc.vector.tensor_copy(out=dst, in_=src)
+                else:
+                    nc.scalar.copy(out=dst, in_=src)
+            nc.vector.quantize_mx(out=xc[b][:, g, :].bitcast(FP8X4), scales=xs[b][:, g, :], in_=t[:, :4 * n])
+
+        def mm1(acc, b, half, t, g):
+            c0 = 512 * half + 128 * t
+            n = 256 * len(class_blocks[b])
+            nc.tensor.matmul_mx(out=acc[:, :n],
+                                lhsT=w1c[:, g, c0:c0 + 128].bitcast(FP8X4),
+                                lhsT_scale=w1s[:, g, c0:c0 + 128],
+                                rhs=xc[b][:, g, :].bitcast(FP8X4),
+                                rhs_scale=xs[b][:, g, :],
+                                start=(g == 0), stop=(g == G1 - 1))
+
+        def new_accs():
+            return [psum.tile([P, 512], F32, name="acc") for t in range(4)]
+
+        def relu(acc, b, half, t):
+            n = 256 * len(class_blocks[b])
+            if t == 0:
+                hp[b, half] = hid.tile([P, 4, 512], BF16, name="hp")
+            nc.scalar.activation(hp[b, half][:, t, :n], acc[:, :n], ACT.Relu, bias=b1c[:, half, t:t + 1])
+
+        def h_prep(b, half, engine):
+            n = 256 * len(class_blocks[b])
+            t = inter.tile([P, 2048], BF16, name="il", align_bytes=64)
+            engine(out=t[:, :4 * n].rearrange("p (n t) -> p n t", t=4),
+                   in_=hp[b, half][:, :, :n].rearrange("p t n -> p n t"))
+            nc.vector.quantize_mx(out=hc[b][:, half, :].bitcast(FP8X4), scales=hs[b][:, half, :], in_=t[:, :4 * n])
+
+        w2r = {}
+
+        def load_w2(g):
+            for c0, c1 in ((0, 512), (512, 768)):
+                t = raw.tile([P, 4, c1 - c0], BF16, name="w1r")
+                nc.sync.dma_start(out=t[:], in_=w2_v[g][:, :, c0:c1])
+                w2r[g, c0] = t
+
+        def w2_prep(g, engine):
+            for c0, c1 in ((0, 512), (512, 768)):
+                t = inter.tile([P, 2048], BF16, name="il", align_bytes=64)
+                n = 4 * (c1 - c0)
+                engine(out=t[:, :n].rearrange("p (c j) -> p c j", j=4),
+                       in_=w2r[g, c0][:].rearrange("p j c -> p c j"))
+                nc.vector.quantize_mx(out=w2c[:, g, c0:c1].bitcast(FP8X4), scales=w2s[:, g, c0:c1], in_=t[:, :n])
+
+        def stage2(b, q):
+            h = class_blocks[b].index(q)
+            mean_sb = outp.tile([P, 2, L], F32, name="mean_sb")
+            std_sb = outp.tile([P, 2, L], F32, name="std_sb")
+            smp = outp.tile([P, 2, L], F32, name="smp")
+            for i in range(2):
+                r0 = 256 * h + 128 * i
+                for part in (1, 0):
+                    ps = psum.tile([P, 512], F32, name="tp")
+                    for c0, c1 in ((0, 256), (256, 384)):
+                        w0, w1_ = L * part + c0, L * part + c1
+                        for g in range(G2):
+                            nc.tensor.matmul_mx(out=ps[:, c0:c1],
+                                                lhsT=hc[b][:, g, r0:r0 + 128].bitcast(FP8X4),
+                                                lhsT_scale=hs[b][:, g, r0:r0 + 128],
+                                                rhs=w2c[:, g, w0:w1_].bitcast(FP8X4),
+                                                rhs_scale=w2s[:, g, w0:w1_],
+                                                start=(g == 0), stop=(g == G2 - 1))
+                    dst = std_sb if part else mean_sb
+                    nc.vector.tensor_add(out=dst[:, i, :], in0=ps[:, :L], in1=b2b[:, L * part:L * part + L])
+                nc.scalar.activation(smp[:, i, :], std_sb[:, i, :], ACT.Sqrt)
+                nc.vector.tensor_mul(out=smp[:, i, :], in0=smp[:, i, :], in1=eps_sb[:, 2 * q + i, :])
+                nc.vector.tensor_add(out=smp[:, i, :], in0=smp[:, i, :], in1=mean_sb[:, i, :])
+            nc.sync.dma_start(out=std_v[:, 2 * q:2 * q + 2, :], in_=std_sb[:])
+            nc.sync.dma_start(out=mean_v[:, 2 * q:2 * q + 2, :], in_=mean_sb[:])
+            nc.sync.dma_start(out=sample_v[:, 2 * q:2 * q + 2, :], in_=smp[:])
+
+        srow = keep.tile([P, P], F32)
+        nc.gpsimd.memset(srow[:], 0.0)
+        nc.sync.dma_start(out=srow[:15, :], in_=obs_scale.rearrange("o (c k) -> (o c) k", k=P))
+        scol = keep.tile([P, 16], F32)
+        tp = psum.tile([P, 512], F32, name="tp")
+        nc.tensor.transpose(tp[:, :P], srow[:], ident[:])
+        nc.scalar.copy(out=scol[:], in_=tp[:, :16])
+        for c0 in range(0, 15, 4):
+            c1 = min(c0 + 4, 15)
+            tp = psum.tile([P, 512], F32, name="tp")
+            for c in range(c0, c1):
+                nc.tensor.transpose(tp[:, P * (c - c0):P * (c - c0 + 1)], scol[:, c:c + 1].to_broadcast([P, P]), ident[:])
+            nc.scalar.copy(out=scale[:, P * c0:P * c1], in_=tp[:, :P * (c1 - c0)])
+
+        new_rows(0)
+        new_rows(1)
+        load_w1(0, 0)
+        load_obs(0)
+        load_state(0, 0, 1)
+        load_state(1, 0, 1)
+        load_w1(0, 1)
+        load_obs(1)
+        load_state(0, 1, 2)
+        load_state(1, 1, 2)
+        for g in range(2, 6):
+            load_w1(0, g)
+        nc.sync.dma_start(out=b1c[:], in_=b1.rearrange("(g p t) -> p g t", p=P, t=4))
+        load_w1(1, 0)
+
+        load_w1(1, 1)
+        new_rows(2)
+        load_obs(2)
+        load_state(2, 0, 2)
+        for g in range(2, 6):
+            load_w1(1, g)
+        load_w2(0)
+        load_w2(1)
+        new_rows(3)
+        load_obs(3)
+        load_state(3, 0, 2)
+        nc.sync.dma_start(out=b2b[:], in_=b2.partition_broadcast(P))
+        nc.sync.dma_start(out=eps_sb[:], in_=eps_v)
+
+        accs = new_accs()
+        for g in range(G1):
+            t = interleave_w1(0, g, 32)
+            if g in (0, 2):
+                c0, c1 = ((0, 896) if g == 0 else (896, 1920))
+                for q in (0, 1):
+                    for i in range(2):
+                        product(q, i, c0, c1)
+            quant_w1(0, g, t)
+            x_prep(0, g, "ss")
+            for tt in range(4):
+                mm1(accs[tt], 0, 0, tt, g)
+        for tt in range(4):
+            relu(accs[tt], 0, 0, tt)
+
+        accs = new_accs()
+        for g in range(G1):
+            t = interleave_w1(1, g, 32)
+            if g == 0:
+                product(2, 0, 0, O)
+            if g == 1:
+                product(2, 1, 0, O)
+            if g == 3:
+                product(3, 0, 0, O)
+            if g == 5:
+                product(3, 1, 0, O)
+            quant_w1(1, g, t)
+            for tt in range(4):
+                mm1(accs[tt], 0, 1, tt, g)
+            x_prep(1, g, "s")
+        for tt in range(4):
+            relu(accs[tt], 0, 1, tt)
+        w2_prep(0, nc.vector.tensor_copy)
+        w2_prep(1, nc.vector.tensor_copy)
+        h_prep(0, 0, nc.vector.tensor_copy)
+        accs = new_accs()
+        for g in range(G1):
+            x_prep(2, g, "s")
+            for tt in range(4):
+                mm1(accs[tt], 1, 0, tt, g)
+            if g == 2:
+                h_prep(0, 1, nc.vector.tensor_copy)
+        for tt in range(4):
+            relu(accs[tt], 1, 0, tt)
+
+        def closed(b, half):
+            for tt in range(4):
+                acc = psum.tile([P, 512], F32, name="acc")
+                for g in range(G1):
+                    mm1(acc, b, half, tt, g)
+                relu(acc, b, half, tt)
+
+        stage2(0, 0)
+        closed(1, 1)
+        h_prep(1, 0, nc.scalar.copy)
+        stage2(0, 1)
+        closed(2, 0)
+        h_prep(1, 1, nc.scalar.copy)
+        closed(2, 1)
+        stage2(1, 2)
+        h_prep(2, 0, nc.scalar.copy)
+        h_prep(2, 1, nc.scalar.copy)
+        stage2(2, 3)

@@ -87,14 +87,11 @@ def tile_rssm_pa_kernel(tc, prev_state, prev_action, obs_bytes, obs_scale, eps,
                                     in0=ob[q][:, i, c0:c1].bitcast(FP8),
                                     in1=scale[:, c0:c1], op=ALU.mult)
 
-        def interleave_w1(half, g, mv):
+        def interleave_w1(half, g, engine):
             t = inter.tile([P, 2048], BF16, name="il", align_bytes=64)
-            dst = t[:].rearrange("p (t m j) -> p m t j", t=4, j=4)
-            src = w1r[half, g][:].rearrange("p j (m t) -> p m t j", t=4)
-            if mv > 0:
-                nc.vector.tensor_copy(out=dst[:, :mv], in_=src[:, :mv])
-            if mv < 128:
-                nc.scalar.copy(out=dst[:, mv:], in_=src[:, mv:])
+            dst = t[:].rearrange("p (t m j) -> p m j t", t=4, j=4)
+            src = w1r[half, g][:].rearrange("p j (m t) -> p m j t", t=4)
+            engine(out=dst, in_=src)
             return t
 
         def quant_w1(half, g, t):
@@ -114,12 +111,11 @@ def tile_rssm_pa_kernel(tc, prev_state, prev_action, obs_bytes, obs_scale, eps,
             hc[b] = keep.tile([P, G2, n], U32, name="hc%d" % b, align_bytes=64)
             hs[b] = keep.tile([P, G2, n], U8, name="hs%d" % b, align_bytes=64)
 
-        def x_prep(b, g, engines):
-            qs = class_blocks[b]
-            n = 256 * len(qs)
+        def x_prep(b, gs):
             t = inter.tile([P, 2048], BF16, name="il", align_bytes=64)
             words_out = t[:].bitcast(F32)
-            for h, q in enumerate(qs):
+            units = [(g, q) for g in gs for q in class_blocks[b]]
+            for h, (g, q) in enumerate(units):
                 tp = psum.tile([P, 2, 256], F32, name="tp")
                 for i in range(2):
                     words = xr[q][:, i, :].bitcast(F32)
@@ -127,12 +123,9 @@ def tile_rssm_pa_kernel(tc, prev_state, prev_action, obs_bytes, obs_scale, eps,
                         nc.tensor.transpose(tp[:, u, 128 * i:128 * i + 128],
                                             words[:, 256 * g + u:256 * g + 256:2], ident[:])
                 dst = words_out[:, 512 * h:512 * h + 512].rearrange("p (r u) -> p r u", u=2)
-                src = tp[:].rearrange("p u r -> p r u")
-                if engines[h] == "v":
-                    nc.vector.tensor_copy(out=dst, in_=src)
-                else:
-                    nc.scalar.copy(out=dst, in_=src)
-            nc.vector.quantize_mx(out=xc[b][:, g, :].bitcast(FP8X4), scales=xs[b][:, g, :], in_=t[:, :4 * n])
+                nc.scalar.copy(out=dst, in_=tp[:].rearrange("p u r -> p r u"))
+            nc.vector.quantize_mx(out=xc[b][:, gs[0]:gs[-1] + 1, :].rearrange("p g n -> p (g n)").bitcast(FP8X4),
+                                  scales=xs[b][:, gs[0]:gs[-1] + 1, :].rearrange("p g n -> p (g n)"), in_=t[:])
 
         def mm1(acc, b, half, t, g):
             c0 = 512 * half + 128 * t
@@ -156,8 +149,8 @@ def tile_rssm_pa_kernel(tc, prev_state, prev_action, obs_bytes, obs_scale, eps,
         def h_prep(b, half, engine):
             n = 256 * len(class_blocks[b])
             t = inter.tile([P, 2048], BF16, name="il", align_bytes=64)
-            engine(out=t[:, :4 * n].rearrange("p (n t) -> p n t", t=4),
-                   in_=hp[b, half][:, :, :n].rearrange("p t n -> p n t"))
+            engine(out=t[:, :4 * n].rearrange("p (c i t) -> p c t i", i=4, t=4),
+                   in_=hp[b, half][:, :, :n].rearrange("p t (c i) -> p c t i", i=4))
             nc.vector.quantize_mx(out=hc[b][:, half, :].bitcast(FP8X4), scales=hs[b][:, half, :], in_=t[:, :4 * n])
 
         w2r = {}
@@ -172,15 +165,21 @@ def tile_rssm_pa_kernel(tc, prev_state, prev_action, obs_bytes, obs_scale, eps,
             for c0, c1 in ((0, 512), (512, 768)):
                 t = inter.tile([P, 2048], BF16, name="il", align_bytes=64)
                 n = 4 * (c1 - c0)
-                engine(out=t[:, :n].rearrange("p (c j) -> p c j", j=4),
-                       in_=w2r[g, c0][:].rearrange("p j c -> p c j"))
+                engine(out=t[:, :n].rearrange("p (c i j) -> p c j i", i=4, j=4),
+                       in_=w2r[g, c0][:].rearrange("p j (c i) -> p c j i", i=4))
                 nc.vector.quantize_mx(out=w2c[:, g, c0:c1].bitcast(FP8X4), scales=w2s[:, g, c0:c1], in_=t[:, :n])
 
-        def stage2(b, q):
+        def stage2(b, q, split):
             h = class_blocks[b].index(q)
             mean_sb = outp.tile([P, 2, L], F32, name="mean_sb")
             std_sb = outp.tile([P, 2, L], F32, name="std_sb")
             smp = outp.tile([P, 2, L], F32, name="smp")
+
+            def sample(s):
+                nc.scalar.activation(smp[:, s, :], std_sb[:, s, :], ACT.Sqrt)
+                nc.vector.tensor_mul(out=smp[:, s, :], in0=smp[:, s, :], in1=eps_sb[:, 2 * q + s.start:2 * q + s.stop, :])
+                nc.vector.tensor_add(out=smp[:, s, :], in0=smp[:, s, :], in1=mean_sb[:, s, :])
+
             for i in range(2):
                 r0 = 256 * h + 128 * i
                 for part in (1, 0):
@@ -196,9 +195,10 @@ def tile_rssm_pa_kernel(tc, prev_state, prev_action, obs_bytes, obs_scale, eps,
                                                 start=(g == 0), stop=(g == G2 - 1))
                     dst = std_sb if part else mean_sb
                     nc.vector.tensor_add(out=dst[:, i, :], in0=ps[:, :L], in1=b2b[:, L * part:L * part + L])
-                nc.scalar.activation(smp[:, i, :], std_sb[:, i, :], ACT.Sqrt)
-                nc.vector.tensor_mul(out=smp[:, i, :], in0=smp[:, i, :], in1=eps_sb[:, 2 * q + i, :])
-                nc.vector.tensor_add(out=smp[:, i, :], in0=smp[:, i, :], in1=mean_sb[:, i, :])
+                if split:
+                    sample(slice(i, i + 1))
+            if not split:
+                sample(slice(0, 2))
             nc.sync.dma_start(out=std_v[:, 2 * q:2 * q + 2, :], in_=std_sb[:])
             nc.sync.dma_start(out=mean_v[:, 2 * q:2 * q + 2, :], in_=mean_sb[:])
             nc.sync.dma_start(out=sample_v[:, 2 * q:2 * q + 2, :], in_=smp[:])
@@ -215,7 +215,8 @@ def tile_rssm_pa_kernel(tc, prev_state, prev_action, obs_bytes, obs_scale, eps,
             tp = psum.tile([P, 512], F32, name="tp")
             for c in range(c0, c1):
                 nc.tensor.transpose(tp[:, P * (c - c0):P * (c - c0 + 1)], scol[:, c:c + 1].to_broadcast([P, P]), ident[:])
-            nc.scalar.copy(out=scale[:, P * c0:P * c1], in_=tp[:, :P * (c1 - c0)])
+            copy = nc.vector.tensor_copy if "SVSS"[c0 // 4] == "V" else nc.scalar.copy
+            copy(out=scale[:, P * c0:P * c1], in_=tp[:, :P * (c1 - c0)])
 
         new_rows(0)
         new_rows(1)
@@ -236,76 +237,314 @@ def tile_rssm_pa_kernel(tc, prev_state, prev_action, obs_bytes, obs_scale, eps,
         new_rows(2)
         load_obs(2)
         load_state(2, 0, 2)
-        for g in range(2, 6):
-            load_w1(1, g)
-        load_w2(0)
-        load_w2(1)
+        load_w1(1, 2)
+        load_w1(1, 3)
         new_rows(3)
         load_obs(3)
         load_state(3, 0, 2)
+        load_w1(1, 4)
+        load_w1(1, 5)
+        load_w2(0)
+        load_w2(1)
         nc.sync.dma_start(out=b2b[:], in_=b2.partition_broadcast(P))
         nc.sync.dma_start(out=eps_sb[:], in_=eps_v)
 
-        accs = new_accs()
-        for g in range(G1):
-            t = interleave_w1(0, g, 32)
-            if g in (0, 2):
-                c0, c1 = ((0, 896) if g == 0 else (896, 1920))
-                for q in (0, 1):
+        vec, sca = nc.vector.tensor_copy, nc.scalar.copy
+        units = [(0, [g]) for g in range(6)] + [(1, [0, 1]), (1, [2, 3]), (1, [4, 5]), (2, [0, 1]), (2, [2, 3]), (2, [4, 5])]
+        tps, wi, xi, accs, hi, w2i, ps, ep = {}, {}, {}, {}, {}, {}, {}, {}
+        ENG = {"V": vec, "S": sca}
+
+        def il(n):
+            wi[n] = interleave_w1(n // 6, n % 6, ENG["VSSSSVSSVVSV"[n]])
+
+        def wq(n):
+            quant_w1(n // 6, n % 6, wi[n])
+
+        def T(u):
+            b, gs = units[u]
+            tps[u] = []
+            for g in gs:
+                for q in class_blocks[b]:
+                    tp = psum.tile([P, 2, 256], F32, name="tp")
                     for i in range(2):
-                        product(q, i, c0, c1)
-            quant_w1(0, g, t)
-            x_prep(0, g, "ss")
-            for tt in range(4):
-                mm1(accs[tt], 0, 0, tt, g)
-        for tt in range(4):
-            relu(accs[tt], 0, 0, tt)
+                        words = xr[q][:, i, :].bitcast(F32)
+                        for w in range(2):
+                            nc.tensor.transpose(tp[:, w, 128 * i:128 * i + 128],
+                                                words[:, 256 * g + w:256 * g + 256:2], ident[:])
+                    tps[u].append(tp)
 
-        accs = new_accs()
-        for g in range(G1):
-            t = interleave_w1(1, g, 32)
+        def Cx(u):
+            t = inter.tile([P, 2048], BF16, name="il", align_bytes=64)
+            for h, tp in enumerate(tps[u]):
+                nc.scalar.copy(out=t[:].bitcast(F32)[:, 512 * h:512 * h + 512].rearrange("p (r u) -> p r u", u=2),
+                               in_=tp[:].rearrange("p u r -> p r u"))
+            xi[u] = t
+
+        def Q(u):
+            b, gs = units[u]
+            nc.vector.quantize_mx(out=xc[b][:, gs[0]:gs[-1] + 1, :].rearrange("p g n -> p (g n)").bitcast(FP8X4),
+                                  scales=xs[b][:, gs[0]:gs[-1] + 1, :].rearrange("p g n -> p (g n)"), in_=xi[u][:])
+
+        def PR(k):
+            if k < 8:
+                product((k // 2) % 2, k % 2, 0 if k < 4 else 896, 896 if k < 4 else O)
+            else:
+                product(2 + (k - 8) // 2, k % 2, 0, O)
+
+        def M(b, half, g):
             if g == 0:
-                product(2, 0, 0, O)
-            if g == 1:
-                product(2, 1, 0, O)
-            if g == 3:
-                product(3, 0, 0, O)
-            if g == 5:
-                product(3, 1, 0, O)
-            quant_w1(1, g, t)
+                accs[b, half] = new_accs()
             for tt in range(4):
-                mm1(accs[tt], 0, 1, tt, g)
-            x_prep(1, g, "s")
-        for tt in range(4):
-            relu(accs[tt], 0, 1, tt)
-        w2_prep(0, nc.vector.tensor_copy)
-        w2_prep(1, nc.vector.tensor_copy)
-        h_prep(0, 0, nc.vector.tensor_copy)
-        accs = new_accs()
-        for g in range(G1):
-            x_prep(2, g, "s")
-            for tt in range(4):
-                mm1(accs[tt], 1, 0, tt, g)
-            if g == 2:
-                h_prep(0, 1, nc.vector.tensor_copy)
-        for tt in range(4):
-            relu(accs[tt], 1, 0, tt)
+                mm1(accs[b, half][tt], b, half, tt, g)
 
-        def closed(b, half):
+        def R(b, half):
             for tt in range(4):
-                acc = psum.tile([P, 512], F32, name="acc")
-                for g in range(G1):
-                    mm1(acc, b, half, tt, g)
-                relu(acc, b, half, tt)
+                relu(accs[b, half][tt], b, half, tt)
 
-        stage2(0, 0)
-        closed(1, 1)
-        h_prep(1, 0, nc.scalar.copy)
-        stage2(0, 1)
-        closed(2, 0)
-        h_prep(1, 1, nc.scalar.copy)
-        closed(2, 1)
-        stage2(1, 2)
-        h_prep(2, 0, nc.scalar.copy)
-        h_prep(2, 1, nc.scalar.copy)
-        stage2(2, 3)
+        def C1(b, half, tt):
+            acc = psum.tile([P, 512], F32, name="acc")
+            for g in range(G1):
+                mm1(acc, b, half, tt, g)
+            accs[b, half, tt] = acc
+
+        def R1(b, half, tt):
+            relu(accs[b, half, tt], b, half, tt)
+
+        def HI(b, half):
+            n = 256 * len(class_blocks[b])
+            t = inter.tile([P, 2048], BF16, name="il", align_bytes=64)
+            ENG[["SS","SS","SS"][b][half]](
+                out=t[:, :4 * n].rearrange("p (c i t) -> p c t i", i=4, t=4),
+                in_=hp[b, half][:, :, :n].rearrange("p t (c i) -> p c t i", i=4))
+            hi[b, half] = t
+
+        def HQ(b, half):
+            n = 256 * len(class_blocks[b])
+            nc.vector.quantize_mx(out=hc[b][:, half, :].bitcast(FP8X4), scales=hs[b][:, half, :], in_=hi[b, half][:, :4 * n])
+
+        def W2RANGE(k):
+            return k // 2, 512 * (k % 2), 512 + 256 * (k % 2)
+
+        def WI(k):
+            g, c0, c1 = W2RANGE(k)
+            t = inter.tile([P, 2048], BF16, name="il", align_bytes=64)
+            ENG["VVVS"[k]](out=t[:, :4 * (c1 - c0)].rearrange("p (c i j) -> p c j i", i=4, j=4),
+                               in_=w2r[g, c0][:].rearrange("p j (c i) -> p c j i", i=4))
+            w2i[k] = t
+
+        def WQ(k):
+            g, c0, c1 = W2RANGE(k)
+            nc.vector.quantize_mx(out=w2c[:, g, c0:c1].bitcast(FP8X4), scales=w2s[:, g, c0:c1], in_=w2i[k][:, :4 * (c1 - c0)])
+
+        def S2(q, i):
+            b = 0 if q < 2 else q - 1
+            r0 = 256 * class_blocks[b].index(q) + 128 * i
+            for part in (1, 0):
+                acc = psum.tile([P, 512], F32, name="tp")
+                for c0, c1 in ((0, 256), (256, 384)):
+                    w0, w9 = L * part + c0, L * part + c1
+                    for g in range(G2):
+                        nc.tensor.matmul_mx(out=acc[:, c0:c1],
+                                            lhsT=hc[b][:, g, r0:r0 + 128].bitcast(FP8X4),
+                                            lhsT_scale=hs[b][:, g, r0:r0 + 128],
+                                            rhs=w2c[:, g, w0:w9].bitcast(FP8X4),
+                                            rhs_scale=w2s[:, g, w0:w9],
+                                            start=(g == 0), stop=(g == G2 - 1))
+                ps[q, i, part] = acc
+
+        def BA(q, i):
+            if q not in ep:
+                mean_sb = outp.tile([P, 2, L], F32, name="mean_sb")
+                std_sb = outp.tile([P, 2, L], F32, name="std_sb")
+                smp = outp.tile([P, 2, L], F32, name="smp")
+                ep[q] = (mean_sb, std_sb, smp)
+            for part in (1, 0):
+                nc.vector.tensor_add(out=ep[q][part][:, i, :], in0=ps[q, i, part][:, :L], in1=b2b[:, L * part:L * part + L])
+
+        def SQ(q, i):
+            nc.scalar.activation(ep[q][2][:, i[0]:i[-1] + 1, :], ep[q][1][:, i[0]:i[-1] + 1, :], ACT.Sqrt)
+
+        def MU(q, i):
+            s = ep[q][2][:, i[0]:i[-1] + 1, :]
+            nc.vector.tensor_mul(out=s, in0=s, in1=eps_sb[:, 2 * q + i[0]:2 * q + i[-1] + 1, :])
+
+        def AD(q, i):
+            s = ep[q][2][:, i[0]:i[-1] + 1, :]
+            nc.vector.tensor_add(out=s, in0=s, in1=ep[q][0][:, i[0]:i[-1] + 1, :])
+
+        def OUT(q):
+            for view, part in ((std_v, 1), (mean_v, 0), (sample_v, 2)):
+                nc.sync.dma_start(out=view[:, 2 * q:2 * q + 2, :], in_=ep[q][part][:])
+
+        with tc.manual_schedule(engines={mybir.EngineType.PE, mybir.EngineType.DVE, mybir.EngineType.Activation}):
+            il(0)
+            T(0)
+            PR(5)
+            PR(0)
+            PR(4)
+            Cx(0)
+            Q(0)
+            PR(1)
+            PR(2)
+            il(1)
+            T(1)
+            wq(0)
+            Cx(1)
+            Q(1)
+            il(2)
+            PR(3)
+            PR(7)
+            wq(1)
+            il(3)
+            il(5)
+            T(2)
+            wq(2)
+            Cx(2)
+            wq(5)
+            T(3)
+            PR(6)
+            Cx(3)
+            il(7)
+            T(4)
+            T(5)
+            il(4)
+            Cx(4)
+            wq(3)
+            Cx(5)
+            PR(9)
+            Q(2)
+            M(0, 0, 0)
+            il(6)
+            PR(8)
+            Q(3)
+            wq(4)
+            M(0, 0, 1)
+            il(8)
+            M(0, 0, 2)
+            Q(4)
+            Q(5)
+            il(11)
+            T(6)
+            Cx(6)
+            wq(7)
+            T(8)
+            M(0, 0, 3)
+            M(0, 0, 4)
+            il(9)
+            wq(6)
+            Cx(8)
+            M(0, 0, 5)
+            wq(11)
+            wq(9)
+            T(9)
+            T(7)
+            R(0, 0)
+            il(10)
+            HI(0, 0)
+            wq(8)
+            M(0, 1, 0)
+            Cx(7)
+            M(0, 1, 1)
+            wq(10)
+            PR(11)
+            M(0, 1, 2)
+            PR(10)
+            M(0, 1, 3)
+            Q(7)
+            Q(6)
+            Q(8)
+            M(0, 1, 4)
+            Cx(9)
+            M(0, 1, 5)
+            T(10)
+            T(11)
+            WI(0)
+            R(0, 1)
+            Cx(11)
+            HQ(0, 0)
+            HI(0, 1)
+            M(1, 0, 0)
+            M(1, 0, 1)
+            M(1, 0, 2)
+            M(1, 0, 3)
+            M(1, 0, 4)
+            WI(1)
+            WI(2)
+            WQ(0)
+            M(1, 0, 5)
+            R(1, 0)
+            HQ(0, 1)
+            C1(1, 1, 3)
+            WI(3)
+            WQ(1)
+            C1(1, 1, 0)
+            Cx(10)
+            R1(1, 1, 0)
+            C1(1, 1, 1)
+            WQ(2)
+            R1(1, 1, 1)
+            WQ(3)
+            C1(1, 1, 2)
+            S2(0, 1)
+            Q(9)
+            Q(11)
+            R1(1, 1, 2)
+            S2(0, 0)
+            BA(0, 1)
+            R1(1, 1, 3)
+            Q(10)
+            HI(1, 0)
+            BA(0, 0)
+            M(2, 0, 0)
+            S2(1, 0)
+            M(2, 0, 1)
+            SQ(0, (0,1))
+            BA(1, 0)
+            M(2, 0, 2)
+            HI(1, 1)
+            MU(0, (0,1))
+            AD(0, (0,1))
+            M(2, 0, 3)
+            M(2, 0, 4)
+            M(2, 0, 5)
+            S2(1, 1)
+            R(2, 0)
+            BA(1, 1)
+            C1(2, 1, 0)
+            OUT(0)
+            C1(2, 1, 1)
+            C1(2, 1, 2)
+            HQ(1, 1)
+            HQ(1, 0)
+            SQ(1, (0,1))
+            C1(2, 1, 3)
+            S2(2, 1)
+            MU(1, (0,1))
+            R1(2, 1, 0)
+            AD(1, (0,1))
+            OUT(1)
+            R1(2, 1, 1)
+            HI(2, 0)
+            HQ(2, 0)
+            BA(2, 1)
+            R1(2, 1, 2)
+            S2(2, 0)
+            R1(2, 1, 3)
+            BA(2, 0)
+            HI(2, 1)
+            SQ(2, (0,1))
+            HQ(2, 1)
+            S2(3, 1)
+            MU(2, (0,1))
+            BA(3, 1)
+            S2(3, 0)
+            BA(3, 0)
+            AD(2, (0,1))
+            OUT(2)
+            SQ(3, (0,))
+            MU(3, (0,))
+            SQ(3, (1,))
+            MU(3, (1,))
+            AD(3, (0,))
+            AD(3, (1,))
+            OUT(3)

from contextlib import ExitStack

import concourse.mybir as mybir
from concourse.masks import make_identity

B, S, A, O, H, L = 1024, 1024, 128, 1920, 1024, 384
K1 = S + A + O
FLOPS = 2 * B * K1 * H + 2 * B * H * 2 * L

F32 = mybir.dt.float32
BF16 = mybir.dt.bfloat16
U32 = mybir.dt.uint32
U8 = mybir.dt.uint8
FP8 = mybir.dt.float8_e4m3fn
FP8X4 = mybir.dt.float8_e4m3fn_x4
ACT = mybir.ActivationFunctionType
ALU = mybir.AluOpType

P = 128
G1 = K1 // 512
G2 = H // 512
NT = B // P


def tile_rssm_pa_kernel(tc, prev_state, prev_action, obs_bytes, obs_scale, eps,
                                    w1, b1, w2, b2, out_mean, out_std, out_sample):
    nc = tc.nc

    state_v = prev_state.rearrange("(p i) k -> p i k", i=NT)
    action_v = prev_action.rearrange("(p i) k -> p i k", i=NT)
    bytes_v = obs_bytes.rearrange("(p i) k -> p i k", i=NT)
    eps_v = eps.rearrange("(p i) n -> p i n", i=NT)
    mean_v = out_mean.rearrange("(p i) n -> p i n", i=NT)
    std_v = out_std.rearrange("(p i) n -> p i n", i=NT)
    sample_v = out_sample.rearrange("(p i) n -> p i n", i=NT)
    w1_v = w1.rearrange("(g p j) c -> g p j c", p=P, j=4)
    w2_v = w2.rearrange("(g p j) c -> g p j c", p=P, j=4)

    with ExitStack() as ctx:
        keep = ctx.enter_context(tc.tile_pool(name="keep", bufs=1))
        rows = ctx.enter_context(tc.tile_pool(name="rows", bufs=3))
        raw = ctx.enter_context(tc.tile_pool(name="raw", bufs=7))
        inter = ctx.enter_context(tc.tile_pool(name="inter", bufs=8))
        hid = ctx.enter_context(tc.tile_pool(name="hid", bufs=2))
        outp = ctx.enter_context(tc.tile_pool(name="outp", bufs=2))
        psum = ctx.enter_context(tc.psum_pool(name="psum", bufs=4))

        ident = keep.tile([P, P], F32)
        make_identity(nc, ident[:])
        warm = keep.tile([P, 1], F32)
        nc.vector.memset(warm[:], 1.0)
        nc.scalar.activation(warm[:], warm[:], ACT.Sqrt)

        w1c = keep.tile([P, G1, H], U32, align_bytes=64)
        w1s = keep.tile([P, G1, H], U8, align_bytes=64)
        w2c = keep.tile([P, G2, 2 * L], U32, align_bytes=64)
        w2s = keep.tile([P, G2, 2 * L], U8, align_bytes=64)
        scale = keep.tile([P, O], F32)
        b1c = keep.tile([P, G2, 4], BF16)
        b2b = keep.tile([P, 2 * L], BF16)
        eps_sb = keep.tile([P, NT, L], BF16)

        xr = {}
        ob = {}
        w1r = {}

        def load_w1(half, g):
            t = raw.tile([P, 4, 512], BF16, name="w1r")
            nc.sync.dma_start(out=t[:], in_=w1_v[g][:, :, 512 * half:512 * half + 512])
            w1r[half, g] = t

        def new_rows(q):
            xr[q] = rows.tile([P, 2, K1], BF16, name="xr", align_bytes=64)

        def load_state(q, g0, g1):
            nc.sync.dma_start(out=xr[q][:, :, 512 * g0:512 * g1],
                              in_=state_v[:, 2 * q:2 * q + 2, 512 * g0:512 * g1])

        def load_obs(q):
            t = rows.tile([P, 2, O], U8, name="ob")
            nc.sync.dma_start(out=t[:], in_=bytes_v[:, 2 * q:2 * q + 2, :])
            ob[q] = t
            nc.sync.dma_start(out=xr[q][:, :, S:S + A], in_=action_v[:, 2 * q:2 * q + 2, :])

        def product(q, i, c0, c1):
            nc.vector.tensor_tensor(out=xr[q][:, i, S + A + c0:S + A + c1],
                                    in0=ob[q][:, i, c0:c1].bitcast(FP8),
                                    in1=scale[:, c0:c1], op=ALU.mult)

        def interleave_w1(half, g, engine):
            t = inter.tile([P, 2048], BF16, name="il", align_bytes=64)
            dst = t[:].rearrange("p (t m j) -> p m j t", t=4, j=4)
            src = w1r[half, g][:].rearrange("p j (m t) -> p m j t", t=4)
            engine(out=dst, in_=src)
            return t

        def quant_w1(half, g, t):
            nc.vector.quantize_mx(out=w1c[:, g, 512 * half:512 * half + 512].bitcast(FP8X4),
                                  scales=w1s[:, g, 512 * half:512 * half + 512], in_=t[:])

        class_blocks = [[0, 1], [2], [3]]
        xc = {}
        xs = {}
        hc = {}
        hs = {}
        hp = {}
        for b, qs in enumerate(class_blocks):
            n = 256 * len(qs)
            xc[b] = keep.tile([P, G1, n], U32, name="xc%d" % b, align_bytes=64)
            xs[b] = keep.tile([P, G1, n], U8, name="xs%d" % b, align_bytes=64)
            hc[b] = keep.tile([P, G2, n], U32, name="hc%d" % b, align_bytes=64)
            hs[b] = keep.tile([P, G2, n], U8, name="hs%d" % b, align_bytes=64)

        def x_prep(b, gs):
            t = inter.tile([P, 2048], BF16, name="il", align_bytes=64)
            words_out = t[:].bitcast(F32)
            units = [(g, q) for g in gs for q in class_blocks[b]]
            for h, (g, q) in enumerate(units):
                tp = psum.tile([P, 2, 256], F32, name="tp")
                for i in range(2):
                    words = xr[q][:, i, :].bitcast(F32)
                    for u in range(2):
                        nc.tensor.transpose(tp[:, u, 128 * i:128 * i + 128],
                                            words[:, 256 * g + u:256 * g + 256:2], ident[:])
                dst = words_out[:, 512 * h:512 * h + 512].rearrange("p (r u) -> p r u", u=2)
                nc.scalar.copy(out=dst, in_=tp[:].rearrange("p u r -> p r u"))
            nc.vector.quantize_mx(out=xc[b][:, gs[0]:gs[-1] + 1, :].rearrange("p g n -> p (g n)").bitcast(FP8X4),
                                  scales=xs[b][:, gs[0]:gs[-1] + 1, :].rearrange("p g n -> p (g n)"), in_=t[:])

        def mm1(acc, b, half, t, g):
            c0 = 512 * half + 128 * t
            n = 256 * len(class_blocks[b])
            nc.tensor.matmul_mx(out=acc[:, :n],
                                lhsT=w1c[:, g, c0:c0 + 128].bitcast(FP8X4),
                                lhsT_scale=w1s[:, g, c0:c0 + 128],
                                rhs=xc[b][:, g, :].bitcast(FP8X4),
                                rhs_scale=xs[b][:, g, :],
                                start=(g == 0), stop=(g == G1 - 1))

        def new_accs():
            return [psum.tile([P, 512], F32, name="acc") for t in range(4)]

        def relu(acc, b, half, t):
            n = 256 * len(class_blocks[b])
            if t == 0:
                hp[b, half] = hid.tile([P, 4, 512], BF16, name="hp")
            nc.scalar.activation(hp[b, half][:, t, :n], acc[:, :n], ACT.Relu, bias=b1c[:, half, t:t + 1])

        def h_prep(b, half, engine):
            n = 256 * len(class_blocks[b])
            t = inter.tile([P, 2048], BF16, name="il", align_bytes=64)
            engine(out=t[:, :4 * n].rearrange("p (c i t) -> p c t i", i=4, t=4),
                   in_=hp[b, half][:, :, :n].rearrange("p t (c i) -> p c t i", i=4))
            nc.vector.quantize_mx(out=hc[b][:, half, :].bitcast(FP8X4), scales=hs[b][:, half, :], in_=t[:, :4 * n])

        w2r = {}

        def load_w2(g):
            for c0, c1 in ((0, 512), (512, 768)):
                t = raw.tile([P, 4, c1 - c0], BF16, name="w1r")
                nc.sync.dma_start(out=t[:], in_=w2_v[g][:, :, c0:c1])
                w2r[g, c0] = t

        def w2_prep(g, engine):
            for c0, c1 in ((0, 512), (512, 768)):
                t = inter.tile([P, 2048], BF16, name="il", align_bytes=64)
                n = 4 * (c1 - c0)
                engine(out=t[:, :n].rearrange("p (c i j) -> p c j i", i=4, j=4),
                       in_=w2r[g, c0][:].rearrange("p j (c i) -> p c j i", i=4))
                nc.vector.quantize_mx(out=w2c[:, g, c0:c1].bitcast(FP8X4), scales=w2s[:, g, c0:c1], in_=t[:, :n])

        def stage2(b, q, split):
            h = class_blocks[b].index(q)
            mean_sb = outp.tile([P, 2, L], F32, name="mean_sb")
            std_sb = outp.tile([P, 2, L], F32, name="std_sb")
            smp = outp.tile([P, 2, L], F32, name="smp")

            def sample(s):
                nc.scalar.activation(smp[:, s, :], std_sb[:, s, :], ACT.Sqrt)
                nc.vector.tensor_mul(out=smp[:, s, :], in0=smp[:, s, :], in1=eps_sb[:, 2 * q + s.start:2 * q + s.stop, :])
                nc.vector.tensor_add(out=smp[:, s, :], in0=smp[:, s, :], in1=mean_sb[:, s, :])

            for i in range(2):
                r0 = 256 * h + 128 * i
                for part in (1, 0):
                    ps = psum.tile([P, 512], F32, name="tp")
                    for c0, c1 in ((0, 256), (256, 384)):
                        w0, w1_ = L * part + c0, L * part + c1
                        for g in range(G2):
                            nc.tensor.matmul_mx(out=ps[:, c0:c1],
                                                lhsT=hc[b][:, g, r0:r0 + 128].bitcast(FP8X4),
                                                lhsT_scale=hs[b][:, g, r0:r0 + 128],
                                                rhs=w2c[:, g, w0:w1_].bitcast(FP8X4),
                                                rhs_scale=w2s[:, g, w0:w1_],
                                                start=(g == 0), stop=(g == G2 - 1))
                    dst = std_sb if part else mean_sb
                    nc.vector.tensor_add(out=dst[:, i, :], in0=ps[:, :L], in1=b2b[:, L * part:L * part + L])
                if split:
                    sample(slice(i, i + 1))
            if not split:
                sample(slice(0, 2))
            nc.sync.dma_start(out=std_v[:, 2 * q:2 * q + 2, :], in_=std_sb[:])
            nc.sync.dma_start(out=mean_v[:, 2 * q:2 * q + 2, :], in_=mean_sb[:])
            nc.sync.dma_start(out=sample_v[:, 2 * q:2 * q + 2, :], in_=smp[:])

        srow = keep.tile([P, P], F32)
        nc.gpsimd.memset(srow[:], 0.0)
        nc.sync.dma_start(out=srow[:15, :], in_=obs_scale.rearrange("o (c k) -> (o c) k", k=P))
        scol = keep.tile([P, 16], F32)
        tp = psum.tile([P, 512], F32, name="tp")
        nc.tensor.transpose(tp[:, :P], srow[:], ident[:])
        nc.scalar.copy(out=scol[:], in_=tp[:, :16])
        for c0 in range(0, 15, 4):
            c1 = min(c0 + 4, 15)
            tp = psum.tile([P, 512], F32, name="tp")
            for c in range(c0, c1):
                nc.tensor.transpose(tp[:, P * (c - c0):P * (c - c0 + 1)], scol[:, c:c + 1].to_broadcast([P, P]), ident[:])
            copy = nc.vector.tensor_copy if "SVSS"[c0 // 4] == "V" else nc.scalar.copy
            copy(out=scale[:, P * c0:P * c1], in_=tp[:, :P * (c1 - c0)])

        new_rows(0)
        new_rows(1)
        load_w1(0, 0)
        load_obs(0)
        load_state(0, 0, 1)
        load_state(1, 0, 1)
        load_w1(0, 1)
        load_obs(1)
        load_state(0, 1, 2)
        load_state(1, 1, 2)
        for g in range(2, 6):
            load_w1(0, g)
        nc.sync.dma_start(out=b1c[:], in_=b1.rearrange("(g p t) -> p g t", p=P, t=4))
        load_w1(1, 0)

        load_w1(1, 1)
        new_rows(2)
        load_obs(2)
        load_state(2, 0, 2)
        load_w1(1, 2)
        load_w1(1, 3)
        new_rows(3)
        load_obs(3)
        load_state(3, 0, 2)
        load_w1(1, 4)
        load_w1(1, 5)
        load_w2(0)
        load_w2(1)
        nc.sync.dma_start(out=b2b[:], in_=b2.partition_broadcast(P))
        nc.sync.dma_start(out=eps_sb[:], in_=eps_v)

        vec, sca = nc.vector.tensor_copy, nc.scalar.copy
        units = [(0, [g]) for g in range(6)] + [(1, [0, 1]), (1, [2, 3]), (1, [4, 5]), (2, [0, 1]), (2, [2, 3]), (2, [4, 5])]
        tps, wi, xi, accs, hi, w2i, ps, ep = {}, {}, {}, {}, {}, {}, {}, {}
        ENG = {"V": vec, "S": sca}

        def il(n):
            wi[n] = interleave_w1(n // 6, n % 6, ENG["VSSSSVSSVVSV"[n]])

        def wq(n):
            quant_w1(n // 6, n % 6, wi[n])

        def T(u):
            b, gs = units[u]
            tps[u] = []
            for g in gs:
                for q in class_blocks[b]:
                    tp = psum.tile([P, 2, 256], F32, name="tp")
                    for i in range(2):
                        words = xr[q][:, i, :].bitcast(F32)
                        for w in range(2):
                            nc.tensor.transpose(tp[:, w, 128 * i:128 * i + 128],
                                                words[:, 256 * g + w:256 * g + 256:2], ident[:])
                    tps[u].append(tp)

        def Cx(u):
            t = inter.tile([P, 2048], BF16, name="il", align_bytes=64)
            for h, tp in enumerate(tps[u]):
                nc.scalar.copy(out=t[:].bitcast(F32)[:, 512 * h:512 * h + 512].rearrange("p (r u) -> p r u", u=2),
                               in_=tp[:].rearrange("p u r -> p r u"))
            xi[u] = t

        def Q(u):
            b, gs = units[u]
            nc.vector.quantize_mx(out=xc[b][:, gs[0]:gs[-1] + 1, :].rearrange("p g n -> p (g n)").bitcast(FP8X4),
                                  scales=xs[b][:, gs[0]:gs[-1] + 1, :].rearrange("p g n -> p (g n)"), in_=xi[u][:])

        def PR(k):
            if k < 8:
                product((k // 2) % 2, k % 2, 0 if k < 4 else 896, 896 if k < 4 else O)
            else:
                product(2 + (k - 8) // 2, k % 2, 0, O)

        def M(b, half, g):
            if g == 0:
                accs[b, half] = new_accs()
            for tt in range(4):
                mm1(accs[b, half][tt], b, half, tt, g)

        def R(b, half):
            for tt in range(4):
                relu(accs[b, half][tt], b, half, tt)

        def C1(b, half, tt):
            acc = psum.tile([P, 512], F32, name="acc")
            for g in range(G1):
                mm1(acc, b, half, tt, g)
            accs[b, half, tt] = acc

        def R1(b, half, tt):
            relu(accs[b, half, tt], b, half, tt)

        def HI(b, half):
            n = 256 * len(class_blocks[b])
            t = inter.tile([P, 2048], BF16, name="il", align_bytes=64)
            ENG[["SS","SS","SS"][b][half]](
                out=t[:, :4 * n].rearrange("p (c i t) -> p c t i", i=4, t=4),
                in_=hp[b, half][:, :, :n].rearrange("p t (c i) -> p c t i", i=4))
            hi[b, half] = t

        def HQ(b, half):
            n = 256 * len(class_blocks[b])
            nc.vector.quantize_mx(out=hc[b][:, half, :].bitcast(FP8X4), scales=hs[b][:, half, :], in_=hi[b, half][:, :4 * n])

        def W2RANGE(k):
            return k // 2, 512 * (k % 2), 512 + 256 * (k % 2)

        def WI(k):
            g, c0, c1 = W2RANGE(k)
            t = inter.tile([P, 2048], BF16, name="il", align_bytes=64)
            ENG["VVVS"[k]](out=t[:, :4 * (c1 - c0)].rearrange("p (c i j) -> p c j i", i=4, j=4),
                               in_=w2r[g, c0][:].rearrange("p j (c i) -> p c j i", i=4))
            w2i[k] = t

        def WQ(k):
            g, c0, c1 = W2RANGE(k)
            nc.vector.quantize_mx(out=w2c[:, g, c0:c1].bitcast(FP8X4), scales=w2s[:, g, c0:c1], in_=w2i[k][:, :4 * (c1 - c0)])

        def S2(q, i):
            b = 0 if q < 2 else q - 1
            r0 = 256 * class_blocks[b].index(q) + 128 * i
            for part in (1, 0):
                acc = psum.tile([P, 512], F32, name="tp")
                for c0, c1 in ((0, 256), (256, 384)):
                    w0, w9 = L * part + c0, L * part + c1
                    for g in range(G2):
                        nc.tensor.matmul_mx(out=acc[:, c0:c1],
                                            lhsT=hc[b][:, g, r0:r0 + 128].bitcast(FP8X4),
                                            lhsT_scale=hs[b][:, g, r0:r0 + 128],
                                            rhs=w2c[:, g, w0:w9].bitcast(FP8X4),
                                            rhs_scale=w2s[:, g, w0:w9],
                                            start=(g == 0), stop=(g == G2 - 1))
                ps[q, i, part] = acc

        def BA(q, i):
            if q not in ep:
                mean_sb = outp.tile([P, 2, L], F32, name="mean_sb")
                std_sb = outp.tile([P, 2, L], F32, name="std_sb")
                smp = outp.tile([P, 2, L], F32, name="smp")
                ep[q] = (mean_sb, std_sb, smp)
            for part in (1, 0):
                nc.vector.tensor_add(out=ep[q][part][:, i, :], in0=ps[q, i, part][:, :L], in1=b2b[:, L * part:L * part + L])

        def SQ(q, i):
            nc.scalar.activation(ep[q][2][:, i[0]:i[-1] + 1, :], ep[q][1][:, i[0]:i[-1] + 1, :], ACT.Sqrt)

        def MU(q, i):
            s = ep[q][2][:, i[0]:i[-1] + 1, :]
            nc.vector.tensor_mul(out=s, in0=s, in1=eps_sb[:, 2 * q + i[0]:2 * q + i[-1] + 1, :])

        def AD(q, i):
            s = ep[q][2][:, i[0]:i[-1] + 1, :]
            nc.vector.tensor_add(out=s, in0=s, in1=ep[q][0][:, i[0]:i[-1] + 1, :])

        def OUT(q):
            for view, part in ((std_v, 1), (mean_v, 0), (sample_v, 2)):
                nc.sync.dma_start(out=view[:, 2 * q:2 * q + 2, :], in_=ep[q][part][:])

        with tc.manual_schedule(engines={mybir.EngineType.PE, mybir.EngineType.DVE, mybir.EngineType.Activation}):
            il(0)
            T(0)
            PR(5)
            PR(0)
            PR(4)
            Cx(0)
            Q(0)
            PR(1)
            PR(2)
            il(1)
            T(1)
            wq(0)
            Cx(1)
            Q(1)
            il(2)
            PR(3)
            PR(7)
            wq(1)
            il(3)
            il(5)
            T(2)
            wq(2)
            Cx(2)
            wq(5)
            T(3)
            PR(6)
            Cx(3)
            il(7)
            T(4)
            T(5)
            il(4)
            Cx(4)
            wq(3)
            Cx(5)
            PR(9)
            Q(2)
            M(0, 0, 0)
            il(6)
            PR(8)
            Q(3)
            wq(4)
            M(0, 0, 1)
            il(8)
            M(0, 0, 2)
            Q(4)
            Q(5)
            il(11)
            T(6)
            Cx(6)
            wq(7)
            T(8)
            M(0, 0, 3)
            M(0, 0, 4)
            il(9)
            wq(6)
            Cx(8)
            M(0, 0, 5)
            wq(11)
            wq(9)
            T(9)
            T(7)
            R(0, 0)
            il(10)
            HI(0, 0)
            wq(8)
            M(0, 1, 0)
            Cx(7)
            M(0, 1, 1)
            wq(10)
            PR(11)
            M(0, 1, 2)
            PR(10)
            M(0, 1, 3)
            Q(7)
            Q(6)
            Q(8)
            M(0, 1, 4)
            Cx(9)
            M(0, 1, 5)
            T(10)
            T(11)
            WI(0)
            R(0, 1)
            Cx(11)
            HQ(0, 0)
            HI(0, 1)
            M(1, 0, 0)
            M(1, 0, 1)
            M(1, 0, 2)
            M(1, 0, 3)
            M(1, 0, 4)
            WI(1)
            WI(2)
            WQ(0)
            M(1, 0, 5)
            R(1, 0)
            HQ(0, 1)
            C1(1, 1, 3)
            WI(3)
            WQ(1)
            C1(1, 1, 0)
            Cx(10)
            R1(1, 1, 0)
            C1(1, 1, 1)
            WQ(2)
            R1(1, 1, 1)
            WQ(3)
            C1(1, 1, 2)
            S2(0, 1)
            Q(9)
            Q(11)
            R1(1, 1, 2)
            S2(0, 0)
            BA(0, 1)
            R1(1, 1, 3)
            Q(10)
            HI(1, 0)
            BA(0, 0)
            M(2, 0, 0)
            S2(1, 0)
            M(2, 0, 1)
            SQ(0, (0,1))
            BA(1, 0)
            M(2, 0, 2)
            HI(1, 1)
            MU(0, (0,1))
            AD(0, (0,1))
            M(2, 0, 3)
            M(2, 0, 4)
            M(2, 0, 5)
            S2(1, 1)
            R(2, 0)
            BA(1, 1)
            C1(2, 1, 0)
            OUT(0)
            C1(2, 1, 1)
            C1(2, 1, 2)
            HQ(1, 1)
            HQ(1, 0)
            SQ(1, (0,1))
            C1(2, 1, 3)
            S2(2, 1)
            MU(1, (0,1))
            R1(2, 1, 0)
            AD(1, (0,1))
            OUT(1)
            R1(2, 1, 1)
            HI(2, 0)
            HQ(2, 0)
            BA(2, 1)
            R1(2, 1, 2)
            S2(2, 0)
            R1(2, 1, 3)
            BA(2, 0)
            HI(2, 1)
            SQ(2, (0,1))
            HQ(2, 1)
            S2(3, 1)
            MU(2, (0,1))
            BA(3, 1)
            S2(3, 0)
            BA(3, 0)
            AD(2, (0,1))
            OUT(2)
            SQ(3, (0,))
            MU(3, (0,))
            SQ(3, (1,))
            MU(3, (1,))
            AD(3, (0,))
            AD(3, (1,))
            OUT(3)
